import numpy as np
import ml_dtypes

BF16 = ml_dtypes.bfloat16


def bf(x):
    return np.asarray(x, np.float32).astype(BF16)


def f32(x):
    return np.asarray(x, np.float32)


def f64(x):
    return np.asarray(x).astype(np.float64)


def striped(idx):
    return np.tile(idx.reshape(-1, 16).T, (8, 1))


V, D, DC, M, N = 4096, 128, 64, 512, 2048
BASE = 10000.0
TMAX = 1.5


def setup_inputs():
    k = np.arange(D)
    return {
        "table": bf(np.random.standard_normal((D, V))),
        "w_tab": bf(np.random.standard_normal((D, M)) / np.sqrt(D)),
        "w_enc": bf(np.random.standard_normal((D, M)) / np.sqrt(DC)),
        "b": f32(0.1 * np.random.standard_normal((M, 1))),
        "t_time": f32(TMAX * np.random.random((1, N))),
        "t_f0": f32(TMAX * np.random.random((1, N))),
        "freq": f32(BASE ** (-(k % DC) / DC)).reshape(D, 1),
        "phase": f32((k % 2) * (np.pi / 2.0)).reshape(D, 1),
        "offs": striped(np.random.permutation(np.tile(np.arange(V), 2))[:N]),
    }


def reference(table, w_tab, w_enc, b, t_time, t_f0, freq, phase, offs):
    idx = offs[:16].T.reshape(-1)
    tt = np.concatenate([np.repeat(f64(t_time), DC, axis=0), np.repeat(f64(t_f0), DC, axis=0)], axis=0)
    enc = np.sin(tt * f64(freq) + f64(phase))
    return f64(w_tab).T @ f64(table)[:, idx] + f64(w_enc).T @ enc + f64(b)

@@ -1,0 +1,113 @@
+import math
+
+import concourse.mybir as mybir
+
+BF16, F32, I32, U16 = mybir.dt.bfloat16, mybir.dt.float32, mybir.dt.int32, mybir.dt.uint16
+MULT, ADD, SUBTRACT = mybir.AluOpType.mult, mybir.AluOpType.add, mybir.AluOpType.subtract
+SIN, IDENTITY = mybir.ActivationFunctionType.Sin, mybir.ActivationFunctionType.Identity
+
+P = 128
+HALF = 64
+V = 4096
+M = 512
+N = 2048
+PIECE = 512
+N_PIECES = N // PIECE
+N_BLOCKS = M // P
+BANKS = 8
+TWO_PI = 2.0 * math.pi
+TWO_PI_BELOW = 6.28318500518798828125
+
+FLOPS = 2 * (P + P) * M * N
+
+
+def tile_sequencemodel_kernel(tc, table, w_tab, w_enc, b, t_time, t_f0, freq, phase, offs, out):
+    nc = tc.nc
+    with (
+        tc.tile_pool(name="held", bufs=1) as held,
+        tc.tile_pool(name="times", bufs=N_PIECES) as times,
+        tc.tile_pool(name="angles", bufs=2) as angles,
+        tc.tile_pool(name="encs", bufs=N_PIECES) as encs,
+        tc.tile_pool(name="staged", bufs=BANKS) as staged,
+        tc.psum_pool(name="banks", bufs=BANKS) as banks,
+    ):
+        freq_sb = held.tile([P, 1], F32, name="freq_sb")
+        nc.sync.dma_start(freq_sb[:], freq)
+        phase_sb = held.tile([P, 1], F32, name="phase_sb")
+        nc.sync.dma_start(phase_sb[:], phase)
+
+        def load_times(piece):
+            cols = slice(piece * PIECE, (piece + 1) * PIECE)
+            tt = times.tile([P, PIECE], F32, name="tt")
+            nc.sync.dma_start(tt[0:HALF, :], t_time[:, cols].broadcast_to([HALF, PIECE]))
+            nc.sync.dma_start(tt[HALF:P, :], t_f0[:, cols].broadcast_to([HALF, PIECE]))
+            return tt
+
+        tts = [load_times(0), load_times(1)]
+        w_enc_sb = held.tile([P, M], BF16, name="w_enc_sb")
+        nc.scalar.dma_start(w_enc_sb[:], w_enc)
+        w_tab_sb = held.tile([P, M], BF16, name="w_tab_sb")
+        nc.scalar.dma_start(w_tab_sb[:], w_tab)
+        offsets = held.tile([P, N // 16], U16, name="offsets")
+        nc.sync.dma_start(offsets[:], offs)
+        table_sb = held.tile([P, V], BF16, name="table_sb")
+        nc.sync.dma_start(table_sb[:], table)
+        bias = held.tile([P, N_BLOCKS], F32, name="bias")
+        with nc.allow_non_contiguous_dma(reason="512 single floats, one for each row of out"):
+            nc.scalar.dma_start(bias[:], b.rearrange("(block p) one -> p (block one)", p=P))
+        tts += [load_times(2), load_times(3)]
+
+        freq_turns = held.tile([P, 1], F32, name="freq_turns")
+        nc.vector.tensor_scalar(freq_turns[:], freq_sb[:], 1.0 / TWO_PI, None, op0=MULT)
+        phase_turns = held.tile([P, 1], F32, name="phase_turns")
+        nc.vector.tensor_scalar(phase_turns[:], phase_sb[:], 1.0 / TWO_PI, None, op0=MULT)
+
+        def encode(piece):
+            turns = angles.tile([P, PIECE], F32, name="turns")
+            nc.gpsimd.tensor_scalar(turns[:], tts[piece][:], freq_turns[:, 0:1], phase_turns[:, 0:1], op0=MULT, op1=ADD)
+            whole = angles.tile([P, PIECE], I32, name="whole")
+            nc.vector.tensor_copy(whole[:], turns[:])
+            part = angles.tile([P, PIECE], F32, name="part")
+            nc.vector.tensor_tensor(part[:], turns[:], whole[:], SUBTRACT)
+            enc = encs.tile([P, PIECE], BF16, name="enc")
+            nc.scalar.activation(enc[:], part[:], SIN, scale=TWO_PI_BELOW)
+            return enc
+
+        def looked_up(piece):
+            return table_sb[:].indirect(offsets[:, piece * (PIECE // 16) : (piece + 1) * (PIECE // 16)])
+
+        def weights(w_sb, block):
+            return w_sb[:, block * P : (block + 1) * P]
+
+        def finish(acc, piece, block):
+            result = staged.tile([P, PIECE], F32, name="result")
+            if block % 2 == 0:
+                nc.scalar.activation(result[:], acc[:], IDENTITY, bias=bias[:, block : block + 1])
+            else:
+                nc.vector.tensor_scalar(result[:], acc[:], bias[:, block : block + 1], None, op0=ADD)
+            nc.sync.dma_start(out[block * P : (block + 1) * P, piece * PIECE : (piece + 1) * PIECE], result[:])
+
+        first, last = (0, 1), (2, 3)
+        tiles_of = {}
+        for piece in first:
+            enc = encode(piece)
+            for block in range(N_BLOCKS):
+                acc = banks.tile([P, PIECE], F32, name="acc")
+                nc.tensor.matmul(acc[:], weights(w_enc_sb, block), enc[:], start=True, stop=False)
+                tiles_of[(piece, block)] = acc
+        for piece in first:
+            for block in range(N_BLOCKS):
+                acc = tiles_of[(piece, block)]
+                nc.tensor.matmul(acc[:], weights(w_tab_sb, block), looked_up(piece), start=False, stop=True)
+                finish(acc, piece, block)
+        for piece in last:
+            for block in range(N_BLOCKS):
+                acc = banks.tile([P, PIECE], F32, name="acc")
+                nc.tensor.matmul(acc[:], weights(w_tab_sb, block), looked_up(piece), start=True, stop=False)
+                tiles_of[(piece, block)] = acc
+        for piece in last:
+            enc = encode(piece)
+            for block in range(N_BLOCKS):
+                acc = tiles_of[(piece, block)]
+                nc.tensor.matmul(acc[:], weights(w_enc_sb, block), enc[:], start=False, stop=True)
+                finish(acc, piece, block)

@@ -1,6 +1,7 @@
 import math
 
 import concourse.mybir as mybir
+from concourse.masks import make_identity
 
 BF16, F32, I32, U16 = mybir.dt.bfloat16, mybir.dt.float32, mybir.dt.int32, mybir.dt.uint16
 MULT, ADD, SUBTRACT = mybir.AluOpType.mult, mybir.AluOpType.add, mybir.AluOpType.subtract
@@ -14,6 +15,7 @@ N = 2048
 PIECE = 512
 N_PIECES = N // PIECE
 N_BLOCKS = M // P
+N_ROWS = N_BLOCKS + 2
 BANKS = 8
 TWO_PI = 2.0 * math.pi
 TWO_PI_BELOW = 6.28318500518798828125
@@ -31,10 +33,10 @@ def tile_sequencemodel_kernel(tc, table, w_tab, w_enc, b, t_time, t_f0, freq, ph
         tc.tile_pool(name="staged", bufs=BANKS) as staged,
         tc.psum_pool(name="banks", bufs=BANKS) as banks,
     ):
-        freq_sb = held.tile([P, 1], F32, name="freq_sb")
-        nc.sync.dma_start(freq_sb[:], freq)
-        phase_sb = held.tile([P, 1], F32, name="phase_sb")
-        nc.sync.dma_start(phase_sb[:], phase)
+        rows = held.tile([N_ROWS, P], F32, name="rows")
+        nc.sync.dma_start(rows[0:N_BLOCKS, :], b.rearrange("(block p) one -> block (p one)", p=P))
+        nc.sync.dma_start(rows[N_BLOCKS : N_BLOCKS + 1, :], freq.rearrange("p one -> one p"))
+        nc.sync.dma_start(rows[N_BLOCKS + 1 : N_ROWS, :], phase.rearrange("p one -> one p"))
 
         def load_times(piece):
             cols = slice(piece * PIECE, (piece + 1) * PIECE)
@@ -43,28 +45,31 @@ def tile_sequencemodel_kernel(tc, table, w_tab, w_enc, b, t_time, t_f0, freq, ph
             nc.sync.dma_start(tt[HALF:P, :], t_f0[:, cols].broadcast_to([HALF, PIECE]))
             return tt
 
-        tts = [load_times(0), load_times(1)]
+        tts = [load_times(0)]
         w_enc_sb = held.tile([P, M], BF16, name="w_enc_sb")
-        nc.scalar.dma_start(w_enc_sb[:], w_enc)
-        w_tab_sb = held.tile([P, M], BF16, name="w_tab_sb")
-        nc.scalar.dma_start(w_tab_sb[:], w_tab)
+        nc.sync.dma_start(w_enc_sb[:], w_enc)
+        tts += [load_times(1)]
         offsets = held.tile([P, N // 16], U16, name="offsets")
         nc.sync.dma_start(offsets[:], offs)
+        w_tab_sb = held.tile([P, M], BF16, name="w_tab_sb")
+        nc.sync.dma_start(w_tab_sb[:], w_tab)
         table_sb = held.tile([P, V], BF16, name="table_sb")
         nc.sync.dma_start(table_sb[:], table)
-        bias = held.tile([P, N_BLOCKS], F32, name="bias")
-        with nc.allow_non_contiguous_dma(reason="512 single floats, one for each row of out"):
-            nc.scalar.dma_start(bias[:], b.rearrange("(block p) one -> p (block one)", p=P))
         tts += [load_times(2), load_times(3)]
 
-        freq_turns = held.tile([P, 1], F32, name="freq_turns")
-        nc.vector.tensor_scalar(freq_turns[:], freq_sb[:], 1.0 / TWO_PI, None, op0=MULT)
-        phase_turns = held.tile([P, 1], F32, name="phase_turns")
-        nc.vector.tensor_scalar(phase_turns[:], phase_sb[:], 1.0 / TWO_PI, None, op0=MULT)
+        identity = held.tile([N_ROWS, N_ROWS], F32, name="identity")
+        make_identity(nc, identity[:])
+        columns = banks.tile([P, PIECE], F32, name="columns", tag="acc")
+        nc.tensor.matmul(columns[:, 0:N_ROWS], rows[:], identity[:], start=True, stop=True)
+        bias = held.tile([P, N_BLOCKS], F32, name="bias")
+        nc.vector.tensor_copy(bias[:], columns[:, 0:N_BLOCKS])
+        in_turns = held.tile([P, 2], F32, name="in_turns")
+        nc.vector.tensor_scalar(in_turns[:], columns[:, N_BLOCKS:N_ROWS], 1.0 / TWO_PI, None, op0=MULT)
+        freq_turns, phase_turns = in_turns[:, 0:1], in_turns[:, 1:2]
 
         def encode(piece):
             turns = angles.tile([P, PIECE], F32, name="turns")
-            nc.gpsimd.tensor_scalar(turns[:], tts[piece][:], freq_turns[:, 0:1], phase_turns[:, 0:1], op0=MULT, op1=ADD)
+            nc.vector.tensor_scalar(turns[:], tts[piece][:], freq_turns, phase_turns, op0=MULT, op1=ADD)
             whole = angles.tile([P, PIECE], I32, name="whole")
             nc.vector.tensor_copy(whole[:], turns[:])
             part = angles.tile([P, PIECE], F32, name="part")

@@ -13,6 +13,7 @@ V = 4096
 M = 512
 N = 2048
 PIECE = 512
+SIDE = PIECE // 2
 N_PIECES = N // PIECE
 N_BLOCKS = M // P
 N_ROWS = N_BLOCKS + 2
@@ -33,29 +34,26 @@ def tile_sequencemodel_kernel(tc, table, w_tab, w_enc, b, t_time, t_f0, freq, ph
         tc.tile_pool(name="staged", bufs=BANKS) as staged,
         tc.psum_pool(name="banks", bufs=BANKS) as banks,
     ):
-        rows = held.tile([N_ROWS, P], F32, name="rows")
-        nc.sync.dma_start(rows[0:N_BLOCKS, :], b.rearrange("(block p) one -> block (p one)", p=P))
-        nc.sync.dma_start(rows[N_BLOCKS : N_BLOCKS + 1, :], freq.rearrange("p one -> one p"))
-        nc.sync.dma_start(rows[N_BLOCKS + 1 : N_ROWS, :], phase.rearrange("p one -> one p"))
-
-        def load_times(piece):
+        offsets = held.tile([P, N // 16], U16, name="offsets")
+        nc.sync.dma_start(offsets[:], offs)
+        table_sb = held.tile([P, V], BF16, name="table_sb")
+        nc.sync.dma_start(table_sb[:], table)
+        w_tab_sb = held.tile([P, M], BF16, name="w_tab_sb")
+        nc.sync.dma_start(w_tab_sb[:], w_tab)
+        w_enc_sb = held.tile([P, M], BF16, name="w_enc_sb")
+        tts = []
+        for piece in range(N_PIECES):
             cols = slice(piece * PIECE, (piece + 1) * PIECE)
             tt = times.tile([P, PIECE], F32, name="tt")
             nc.sync.dma_start(tt[0:HALF, :], t_time[:, cols].broadcast_to([HALF, PIECE]))
             nc.sync.dma_start(tt[HALF:P, :], t_f0[:, cols].broadcast_to([HALF, PIECE]))
-            return tt
-
-        tts = [load_times(0)]
-        w_enc_sb = held.tile([P, M], BF16, name="w_enc_sb")
-        nc.sync.dma_start(w_enc_sb[:], w_enc)
-        tts += [load_times(1)]
-        offsets = held.tile([P, N // 16], U16, name="offsets")
-        nc.sync.dma_start(offsets[:], offs)
-        w_tab_sb = held.tile([P, M], BF16, name="w_tab_sb")
-        nc.sync.dma_start(w_tab_sb[:], w_tab)
-        table_sb = held.tile([P, V], BF16, name="table_sb")
-        nc.sync.dma_start(table_sb[:], table)
-        tts += [load_times(2), load_times(3)]
+            tts.append(tt)
+            if piece == 0:
+                nc.sync.dma_start(w_enc_sb[:], w_enc)
+        rows = held.tile([N_ROWS, P], F32, name="rows")
+        nc.scalar.dma_start(rows[N_BLOCKS : N_BLOCKS + 1, :], freq.rearrange("p one -> one p"))
+        nc.scalar.dma_start(rows[N_BLOCKS + 1 : N_ROWS, :], phase.rearrange("p one -> one p"))
+        nc.scalar.dma_start(rows[0:N_BLOCKS, :], b.rearrange("(block p) one -> block (p one)", p=P))
 
         identity = held.tile([N_ROWS, N_ROWS], F32, name="identity")
         make_identity(nc, identity[:])
@@ -78,11 +76,20 @@ def tile_sequencemodel_kernel(tc, table, w_tab, w_enc, b, t_time, t_f0, freq, ph
             nc.scalar.activation(enc[:], part[:], SIN, scale=TWO_PI_BELOW)
             return enc
 
-        def looked_up(piece):
-            return table_sb[:].indirect(offsets[:, piece * (PIECE // 16) : (piece + 1) * (PIECE // 16)])
+        def gathered_product(acc, piece, block, opens):
+            looked_up = table_sb[:].indirect(offsets[:, piece * (PIECE // 16) : (piece + 1) * (PIECE // 16)])
+            nc.tensor.matmul(acc[:], w_tab_sb[:, block * P : (block + 1) * P], looked_up, start=opens, stop=not opens)
 
-        def weights(w_sb, block):
-            return w_sb[:, block * P : (block + 1) * P]
+        def enc_product(acc, enc, block, opens):
+            for side in range(2):
+                cols = slice(side * SIDE, (side + 1) * SIDE)
+                nc.tensor.matmul(
+                    acc[:, cols],
+                    w_enc_sb[:, block * P : (block + 1) * P],
+                    enc[:, cols],
+                    start=opens and side == 0,
+                    stop=not opens and side == 1,
+                )
 
         def finish(acc, piece, block):
             result = staged.tile([P, PIECE], F32, name="result")
@@ -92,27 +99,19 @@ def tile_sequencemodel_kernel(tc, table, w_tab, w_enc, b, t_time, t_f0, freq, ph
                 nc.vector.tensor_scalar(result[:], acc[:], bias[:, block : block + 1], None, op0=ADD)
             nc.sync.dma_start(out[block * P : (block + 1) * P, piece * PIECE : (piece + 1) * PIECE], result[:])
 
-        first, last = (0, 1), (2, 3)
-        tiles_of = {}
-        for piece in first:
-            enc = encode(piece)
-            for block in range(N_BLOCKS):
-                acc = banks.tile([P, PIECE], F32, name="acc")
-                nc.tensor.matmul(acc[:], weights(w_enc_sb, block), enc[:], start=True, stop=False)
-                tiles_of[(piece, block)] = acc
-        for piece in first:
-            for block in range(N_BLOCKS):
-                acc = tiles_of[(piece, block)]
-                nc.tensor.matmul(acc[:], weights(w_tab_sb, block), looked_up(piece), start=False, stop=True)
-                finish(acc, piece, block)
-        for piece in last:
-            for block in range(N_BLOCKS):
-                acc = banks.tile([P, PIECE], F32, name="acc")
-                nc.tensor.matmul(acc[:], weights(w_tab_sb, block), looked_up(piece), start=True, stop=False)
-                tiles_of[(piece, block)] = acc
-        for piece in last:
-            enc = encode(piece)
-            for block in range(N_BLOCKS):
-                acc = tiles_of[(piece, block)]
-                nc.tensor.matmul(acc[:], weights(w_enc_sb, block), enc[:], start=False, stop=True)
-                finish(acc, piece, block)
+        tiles = [(piece, block) for piece in range(N_PIECES) for block in range(N_BLOCKS)]
+        first, second = tiles[:BANKS], tiles[BANKS:]
+        accs = {}
+        for piece, block in first:
+            accs[(piece, block)] = banks.tile([P, PIECE], F32, name="acc")
+            gathered_product(accs[(piece, block)], piece, block, opens=True)
+        encs_of = [encode(piece) for piece in range(N_PIECES)]
+        for piece, block in first:
+            enc_product(accs[(piece, block)], encs_of[piece], block, opens=False)
+            finish(accs[(piece, block)], piece, block)
+        for piece, block in second:
+            accs[(piece, block)] = banks.tile([P, PIECE], F32, name="acc")
+            enc_product(accs[(piece, block)], encs_of[piece], block, opens=True)
+        for piece, block in second:
+            gathered_product(accs[(piece, block)], piece, block, opens=False)
+            finish(accs[(piece, block)], piece, block)

@@ -17,6 +17,7 @@ SIDE = PIECE // 2
 N_PIECES = N // PIECE
 N_BLOCKS = M // P
 N_ROWS = N_BLOCKS + 2
+N_WARM = 12
 BANKS = 8
 TWO_PI = 2.0 * math.pi
 TWO_PI_BELOW = 6.28318500518798828125
@@ -54,6 +55,12 @@ def tile_sequencemodel_kernel(tc, table, w_tab, w_enc, b, t_time, t_f0, freq, ph
         nc.scalar.dma_start(rows[N_BLOCKS : N_BLOCKS + 1, :], freq.rearrange("p one -> one p"))
         nc.scalar.dma_start(rows[N_BLOCKS + 1 : N_ROWS, :], phase.rearrange("p one -> one p"))
         nc.scalar.dma_start(rows[0:N_BLOCKS, :], b.rearrange("(block p) one -> block (p one)", p=P))
+
+        zeros = held.tile([P, PIECE], BF16, name="zeros")
+        nc.vector.memset(zeros[:], 0.0)
+        unread = banks.tile([P, PIECE], F32, name="unread", tag="acc")
+        for repeat in range(N_WARM):
+            nc.tensor.matmul(unread[:], zeros[:, 0:P], zeros[:], start=True, stop=True)
 
         identity = held.tile([N_ROWS, N_ROWS], F32, name="identity")
         make_identity(nc, identity[:])

@@ -17,7 +17,6 @@ SIDE = PIECE // 2
 N_PIECES = N // PIECE
 N_BLOCKS = M // P
 N_ROWS = N_BLOCKS + 2
-N_WARM = 12
 BANKS = 8
 TWO_PI = 2.0 * math.pi
 TWO_PI_BELOW = 6.28318500518798828125
@@ -56,12 +55,6 @@ def tile_sequencemodel_kernel(tc, table, w_tab, w_enc, b, t_time, t_f0, freq, ph
         nc.scalar.dma_start(rows[N_BLOCKS + 1 : N_ROWS, :], phase.rearrange("p one -> one p"))
         nc.scalar.dma_start(rows[0:N_BLOCKS, :], b.rearrange("(block p) one -> block (p one)", p=P))
 
-        zeros = held.tile([P, PIECE], BF16, name="zeros")
-        nc.vector.memset(zeros[:], 0.0)
-        unread = banks.tile([P, PIECE], F32, name="unread", tag="acc")
-        for repeat in range(N_WARM):
-            nc.tensor.matmul(unread[:], zeros[:, 0:P], zeros[:], start=True, stop=True)
-
         identity = held.tile([N_ROWS, N_ROWS], F32, name="identity")
         make_identity(nc, identity[:])
         columns = banks.tile([P, PIECE], F32, name="columns", tag="acc")
@@ -74,7 +67,7 @@ def tile_sequencemodel_kernel(tc, table, w_tab, w_enc, b, t_time, t_f0, freq, ph
 
         def encode(piece):
             turns = angles.tile([P, PIECE], F32, name="turns")
-            nc.vector.tensor_scalar(turns[:], tts[piece][:], freq_turns, phase_turns, op0=MULT, op1=ADD)
+            nc.gpsimd.tensor_scalar(turns[:], tts[piece][:], freq_turns, phase_turns, op0=MULT, op1=ADD)
             whole = angles.tile([P, PIECE], I32, name="whole")
             nc.vector.tensor_copy(whole[:], turns[:])
             part = angles.tile([P, PIECE], F32, name="part")

@@ -3,8 +3,9 @@ import math
 import concourse.mybir as mybir
 from concourse.masks import make_identity
 
-BF16, F32, I32, U16 = mybir.dt.bfloat16, mybir.dt.float32, mybir.dt.int32, mybir.dt.uint16
-MULT, ADD, SUBTRACT = mybir.AluOpType.mult, mybir.AluOpType.add, mybir.AluOpType.subtract
+BF16, F32, I32 = mybir.dt.bfloat16, mybir.dt.float32, mybir.dt.int32
+U16, U32 = mybir.dt.uint16, mybir.dt.uint32
+MULT, ADD, AND = mybir.AluOpType.mult, mybir.AluOpType.add, mybir.AluOpType.bitwise_and
 SIN, IDENTITY = mybir.ActivationFunctionType.Sin, mybir.ActivationFunctionType.Identity
 
 P = 128
@@ -20,6 +21,7 @@ N_ROWS = N_BLOCKS + 2
 BANKS = 8
 TWO_PI = 2.0 * math.pi
 TWO_PI_BELOW = 6.28318500518798828125
+STEPS = 1 << 24
 
 FLOPS = 2 * (P + P) * M * N
 
@@ -61,19 +63,17 @@ def tile_sequencemodel_kernel(tc, table, w_tab, w_enc, b, t_time, t_f0, freq, ph
         nc.tensor.matmul(columns[:, 0:N_ROWS], rows[:], identity[:], start=True, stop=True)
         bias = held.tile([P, N_BLOCKS], F32, name="bias")
         nc.vector.tensor_copy(bias[:], columns[:, 0:N_BLOCKS])
-        in_turns = held.tile([P, 2], F32, name="in_turns")
-        nc.vector.tensor_scalar(in_turns[:], columns[:, N_BLOCKS:N_ROWS], 1.0 / TWO_PI, None, op0=MULT)
-        freq_turns, phase_turns = in_turns[:, 0:1], in_turns[:, 1:2]
+        in_steps = held.tile([P, 2], F32, name="in_steps")
+        nc.vector.tensor_scalar(in_steps[:], columns[:, N_BLOCKS:N_ROWS], STEPS / TWO_PI, None, op0=MULT)
+        freq_steps, phase_steps = in_steps[:, 0:1], in_steps[:, 1:2]
 
         def encode(piece):
-            turns = angles.tile([P, PIECE], F32, name="turns")
-            nc.gpsimd.tensor_scalar(turns[:], tts[piece][:], freq_turns, phase_turns, op0=MULT, op1=ADD)
-            whole = angles.tile([P, PIECE], I32, name="whole")
-            nc.vector.tensor_copy(whole[:], turns[:])
-            part = angles.tile([P, PIECE], F32, name="part")
-            nc.vector.tensor_tensor(part[:], turns[:], whole[:], SUBTRACT)
+            angle = angles.tile([P, PIECE], I32, name="angle")
+            nc.vector.tensor_scalar(angle[:], tts[piece][:], freq_steps, phase_steps, op0=MULT, op1=ADD)
+            low = angles.tile([P, PIECE], I32, name="low")
+            nc.vector.tensor_single_scalar(low[:], angle[:], STEPS - 1, op=AND)
             enc = encs.tile([P, PIECE], BF16, name="enc")
-            nc.scalar.activation(enc[:], part[:], SIN, scale=TWO_PI_BELOW)
+            nc.scalar.activation(enc[:], low[:].bitcast(U32), SIN, bias=TWO_PI_BELOW / 2.0, scale=-TWO_PI_BELOW / STEPS)
             return enc
 
         def gathered_product(acc, piece, block, opens):

@@ -1,11 +1,8 @@
-import math
-
 import concourse.mybir as mybir
 from concourse.masks import make_identity
 
-BF16, F32, I32 = mybir.dt.bfloat16, mybir.dt.float32, mybir.dt.int32
-U16, U32 = mybir.dt.uint16, mybir.dt.uint32
-MULT, ADD, AND = mybir.AluOpType.mult, mybir.AluOpType.add, mybir.AluOpType.bitwise_and
+BF16, F32, U16 = mybir.dt.bfloat16, mybir.dt.float32, mybir.dt.uint16
+ADD = mybir.AluOpType.add
 SIN, IDENTITY = mybir.ActivationFunctionType.Sin, mybir.ActivationFunctionType.Identity
 
 P = 128
@@ -19,9 +16,6 @@ N_PIECES = N // PIECE
 N_BLOCKS = M // P
 N_ROWS = N_BLOCKS + 2
 BANKS = 8
-TWO_PI = 2.0 * math.pi
-TWO_PI_BELOW = 6.28318500518798828125
-STEPS = 1 << 24
 
 FLOPS = 2 * (P + P) * M * N
 
@@ -31,7 +25,6 @@ def tile_sequencemodel_kernel(tc, table, w_tab, w_enc, b, t_time, t_f0, freq, ph
     with (
         tc.tile_pool(name="held", bufs=1) as held,
         tc.tile_pool(name="times", bufs=N_PIECES) as times,
-        tc.tile_pool(name="angles", bufs=2) as angles,
         tc.tile_pool(name="encs", bufs=N_PIECES) as encs,
         tc.tile_pool(name="staged", bufs=BANKS) as staged,
         tc.psum_pool(name="banks", bufs=BANKS) as banks,
@@ -61,19 +54,14 @@ def tile_sequencemodel_kernel(tc, table, w_tab, w_enc, b, t_time, t_f0, freq, ph
         make_identity(nc, identity[:])
         columns = banks.tile([P, PIECE], F32, name="columns", tag="acc")
         nc.tensor.matmul(columns[:, 0:N_ROWS], rows[:], identity[:], start=True, stop=True)
-        bias = held.tile([P, N_BLOCKS], F32, name="bias")
-        nc.vector.tensor_copy(bias[:], columns[:, 0:N_BLOCKS])
-        in_steps = held.tile([P, 2], F32, name="in_steps")
-        nc.vector.tensor_scalar(in_steps[:], columns[:, N_BLOCKS:N_ROWS], STEPS / TWO_PI, None, op0=MULT)
-        freq_steps, phase_steps = in_steps[:, 0:1], in_steps[:, 1:2]
+        small = held.tile([P, N_ROWS], F32, name="small")
+        nc.vector.tensor_copy(small[:], columns[:, 0:N_ROWS])
+        bias = small[:, 0:N_BLOCKS]
+        freq_col, phase_col = small[:, N_BLOCKS : N_BLOCKS + 1], small[:, N_BLOCKS + 1 : N_ROWS]
 
         def encode(piece):
-            angle = angles.tile([P, PIECE], I32, name="angle")
-            nc.vector.tensor_scalar(angle[:], tts[piece][:], freq_steps, phase_steps, op0=MULT, op1=ADD)
-            low = angles.tile([P, PIECE], I32, name="low")
-            nc.vector.tensor_single_scalar(low[:], angle[:], STEPS - 1, op=AND)
             enc = encs.tile([P, PIECE], BF16, name="enc")
-            nc.scalar.activation(enc[:], low[:].bitcast(U32), SIN, bias=TWO_PI_BELOW / 2.0, scale=-TWO_PI_BELOW / STEPS)
+            nc.scalar.activation(enc[:], tts[piece][:], SIN, bias=phase_col, scale=freq_col)
             return enc
 
         def gathered_product(acc, piece, block, opens):

@@ -6,7 +6,7 @@ ADD = mybir.AluOpType.add
 SIN, IDENTITY = mybir.ActivationFunctionType.Sin, mybir.ActivationFunctionType.Identity
 
 P = 128
-HALF = 64
+SQUARE = 32
 V = 4096
 M = 512
 N = 2048
@@ -24,7 +24,7 @@ def tile_sequencemodel_kernel(tc, table, w_tab, w_enc, b, t_time, t_f0, freq, ph
     nc = tc.nc
     with (
         tc.tile_pool(name="held", bufs=1) as held,
-        tc.tile_pool(name="times", bufs=N_PIECES) as times,
+        tc.tile_pool(name="times", bufs=2) as times,
         tc.tile_pool(name="encs", bufs=N_PIECES) as encs,
         tc.tile_pool(name="staged", bufs=BANKS) as staged,
         tc.psum_pool(name="banks", bufs=BANKS) as banks,
@@ -35,16 +35,15 @@ def tile_sequencemodel_kernel(tc, table, w_tab, w_enc, b, t_time, t_f0, freq, ph
         nc.sync.dma_start(table_sb[:], table)
         w_tab_sb = held.tile([P, M], BF16, name="w_tab_sb")
         nc.sync.dma_start(w_tab_sb[:], w_tab)
+        runs = held.tile([P, 2 * SQUARE], F32, name="runs", align_bytes=64)
+        for group in range(P // SQUARE):
+            source = t_time if group < 2 else t_f0
+            nc.sync.dma_start(
+                runs[group * SQUARE : (group + 1) * SQUARE, :].rearrange("a (h r) -> a h r", h=2),
+                source.rearrange("one (h a r) -> (one a) h r", h=2, a=SQUARE),
+            )
         w_enc_sb = held.tile([P, M], BF16, name="w_enc_sb")
-        tts = []
-        for piece in range(N_PIECES):
-            cols = slice(piece * PIECE, (piece + 1) * PIECE)
-            tt = times.tile([P, PIECE], F32, name="tt")
-            nc.sync.dma_start(tt[0:HALF, :], t_time[:, cols].broadcast_to([HALF, PIECE]))
-            nc.sync.dma_start(tt[HALF:P, :], t_f0[:, cols].broadcast_to([HALF, PIECE]))
-            tts.append(tt)
-            if piece == 0:
-                nc.sync.dma_start(w_enc_sb[:], w_enc)
+        nc.sync.dma_start(w_enc_sb[:], w_enc)
         rows = held.tile([N_ROWS, P], F32, name="rows")
         nc.scalar.dma_start(rows[N_BLOCKS : N_BLOCKS + 1, :], freq.rearrange("p one -> one p"))
         nc.scalar.dma_start(rows[N_BLOCKS + 1 : N_ROWS, :], phase.rearrange("p one -> one p"))
@@ -59,9 +58,25 @@ def tile_sequencemodel_kernel(tc, table, w_tab, w_enc, b, t_time, t_f0, freq, ph
         bias = small[:, 0:N_BLOCKS]
         freq_col, phase_col = small[:, N_BLOCKS : N_BLOCKS + 1], small[:, N_BLOCKS + 1 : N_ROWS]
 
+        turned = held.tile([P, 2 * SQUARE], F32, name="turned", align_bytes=64)
+        for h in range(2):
+            cols = slice(h * SQUARE, (h + 1) * SQUARE)
+            nc.vector.transpose(turned[:, cols], runs[:, cols])
+
+        def spread(piece):
+            n_runs = PIECE // SQUARE
+            repeated = times.tile([P, PIECE], F32, name="repeated", align_bytes=64)
+            nc.vector.tensor_copy(
+                repeated[:].rearrange("p (c s) -> p c s", s=SQUARE),
+                turned[:, piece * n_runs : (piece + 1) * n_runs].unsqueeze(2).to_broadcast([P, n_runs, SQUARE]),
+            )
+            tt = times.tile([P, PIECE], F32, name="tt", align_bytes=64)
+            nc.vector.transpose(tt[:], repeated[:])
+            return tt
+
         def encode(piece):
             enc = encs.tile([P, PIECE], BF16, name="enc")
-            nc.scalar.activation(enc[:], tts[piece][:], SIN, bias=phase_col, scale=freq_col)
+            nc.scalar.activation(enc[:], spread(piece)[:], SIN, bias=phase_col, scale=freq_col)
             return enc
 
         def gathered_product(acc, piece, block, opens):

@@ -29,12 +29,13 @@ def tile_sequencemodel_kernel(tc, table, w_tab, w_enc, b, t_time, t_f0, freq, ph
         tc.tile_pool(name="staged", bufs=BANKS) as staged,
         tc.psum_pool(name="banks", bufs=BANKS) as banks,
     ):
-        offsets = held.tile([P, N // 16], U16, name="offsets")
-        nc.sync.dma_start(offsets[:], offs)
         table_sb = held.tile([P, V], BF16, name="table_sb")
         nc.sync.dma_start(table_sb[:], table)
+        offsets = held.tile([P, N // 16], U16, name="offsets")
+        nc.sync.dma_start(offsets[:], offs)
         w_tab_sb = held.tile([P, M], BF16, name="w_tab_sb")
-        nc.sync.dma_start(w_tab_sb[:], w_tab)
+        nc.scalar.dma_start(w_tab_sb[:, 0:P], w_tab[:, 0:P])
+        nc.sync.dma_start(w_tab_sb[:, P:M], w_tab[:, P:M])
         runs = held.tile([P, 2 * SQUARE], F32, name="runs", align_bytes=64)
         for group in range(P // SQUARE):
             source = t_time if group < 2 else t_f0

@@ -1,5 +1,4 @@
 import concourse.mybir as mybir
-from concourse.masks import make_identity
 
 BF16, F32, U16 = mybir.dt.bfloat16, mybir.dt.float32, mybir.dt.uint16
 ADD = mybir.AluOpType.add
@@ -14,7 +13,6 @@ PIECE = 512
 SIDE = PIECE // 2
 N_PIECES = N // PIECE
 N_BLOCKS = M // P
-N_ROWS = N_BLOCKS + 2
 BANKS = 8
 
 FLOPS = 2 * (P + P) * M * N
@@ -45,19 +43,12 @@ def tile_sequencemodel_kernel(tc, table, w_tab, w_enc, b, t_time, t_f0, freq, ph
             )
         w_enc_sb = held.tile([P, M], BF16, name="w_enc_sb")
         nc.sync.dma_start(w_enc_sb[:], w_enc)
-        rows = held.tile([N_ROWS, P], F32, name="rows")
-        nc.scalar.dma_start(rows[N_BLOCKS : N_BLOCKS + 1, :], freq.rearrange("p one -> one p"))
-        nc.scalar.dma_start(rows[N_BLOCKS + 1 : N_ROWS, :], phase.rearrange("p one -> one p"))
-        nc.scalar.dma_start(rows[0:N_BLOCKS, :], b.rearrange("(block p) one -> block (p one)", p=P))
-
-        identity = held.tile([N_ROWS, N_ROWS], F32, name="identity")
-        make_identity(nc, identity[:])
-        columns = banks.tile([P, PIECE], F32, name="columns", tag="acc")
-        nc.tensor.matmul(columns[:, 0:N_ROWS], rows[:], identity[:], start=True, stop=True)
-        small = held.tile([P, N_ROWS], F32, name="small")
-        nc.vector.tensor_copy(small[:], columns[:, 0:N_ROWS])
-        bias = small[:, 0:N_BLOCKS]
-        freq_col, phase_col = small[:, N_BLOCKS : N_BLOCKS + 1], small[:, N_BLOCKS + 1 : N_ROWS]
+        freq_col = held.tile([P, 1], F32, name="freq_col")
+        nc.scalar.dma_start(freq_col[:], freq)
+        phase_col = held.tile([P, 1], F32, name="phase_col")
+        nc.scalar.dma_start(phase_col[:], phase)
+        bias = held.tile([P, N_BLOCKS], F32, name="bias")
+        nc.scalar.dma_start(bias[:], b.rearrange("(block p) one -> p (block one)", p=P))
 
         turned = held.tile([P, 2 * SQUARE], F32, name="turned", align_bytes=64)
         for h in range(2):
@@ -77,7 +68,7 @@ def tile_sequencemodel_kernel(tc, table, w_tab, w_enc, b, t_time, t_f0, freq, ph
 
         def encode(piece):
             enc = encs.tile([P, PIECE], BF16, name="enc")
-            nc.scalar.activation(enc[:], spread(piece)[:], SIN, bias=phase_col, scale=freq_col)
+            nc.scalar.activation(enc[:], spread(piece)[:], SIN, bias=phase_col[:], scale=freq_col[:])
             return enc
 
         def gathered_product(acc, piece, block, opens):

@@ -33,6 +33,10 @@ def tile_sequencemodel_kernel(tc, table, w_tab, w_enc, b, t_time, t_f0, freq, ph
         nc.sync.dma_start(offsets[:], offs)
         w_tab_sb = held.tile([P, M], BF16, name="w_tab_sb")
         nc.scalar.dma_start(w_tab_sb[:, 0:P], w_tab[:, 0:P])
+        freq_col = held.tile([P, 1], F32, name="freq_col")
+        nc.sync.dma_start(freq_col[:], freq)
+        phase_col = held.tile([P, 1], F32, name="phase_col")
+        nc.sync.dma_start(phase_col[:], phase)
         nc.sync.dma_start(w_tab_sb[:, P:M], w_tab[:, P:M])
         runs = held.tile([P, 2 * SQUARE], F32, name="runs", align_bytes=64)
         for group in range(P // SQUARE):
@@ -43,12 +47,8 @@ def tile_sequencemodel_kernel(tc, table, w_tab, w_enc, b, t_time, t_f0, freq, ph
             )
         w_enc_sb = held.tile([P, M], BF16, name="w_enc_sb")
         nc.sync.dma_start(w_enc_sb[:], w_enc)
-        freq_col = held.tile([P, 1], F32, name="freq_col")
-        nc.scalar.dma_start(freq_col[:], freq)
-        phase_col = held.tile([P, 1], F32, name="phase_col")
-        nc.scalar.dma_start(phase_col[:], phase)
         bias = held.tile([P, N_BLOCKS], F32, name="bias")
-        nc.scalar.dma_start(bias[:], b.rearrange("(block p) one -> p (block one)", p=P))
+        nc.sync.dma_start(bias[:], b.rearrange("(block p) one -> p (block one)", p=P))
 
         turned = held.tile([P, 2 * SQUARE], F32, name="turned", align_bytes=64)
         for h in range(2):

@@ -10,7 +10,6 @@ V = 4096
 M = 512
 N = 2048
 PIECE = 512
-SIDE = PIECE // 2
 N_PIECES = N // PIECE
 N_BLOCKS = M // P
 BANKS = 8
@@ -76,14 +75,16 @@ def tile_sequencemodel_kernel(tc, table, w_tab, w_enc, b, t_time, t_f0, freq, ph
             nc.tensor.matmul(acc[:], w_tab_sb[:, block * P : (block + 1) * P], looked_up, start=opens, stop=not opens)
 
         def enc_product(acc, enc, block, opens):
-            for side in range(2):
-                cols = slice(side * SIDE, (side + 1) * SIDE)
+            n_cuts = 1 if opens else 2
+            width = PIECE // n_cuts
+            for cut in range(n_cuts):
+                cols = slice(cut * width, (cut + 1) * width)
                 nc.tensor.matmul(
                     acc[:, cols],
                     w_enc_sb[:, block * P : (block + 1) * P],
                     enc[:, cols],
-                    start=opens and side == 0,
-                    stop=not opens and side == 1,
+                    start=opens,
+                    stop=not opens and cut == n_cuts - 1,
                 )
 
         def finish(acc, piece, block):

@@ -88,12 +88,17 @@ def tile_sequencemodel_kernel(tc, table, w_tab, w_enc, b, t_time, t_f0, freq, ph
                 )
 
         def finish(acc, piece, block):
+            n_cuts = 2 if (piece, block) == (N_PIECES - 1, N_BLOCKS - 1) else 1
+            width = PIECE // n_cuts
             result = staged.tile([P, PIECE], F32, name="result")
-            if block % 2 == 0:
-                nc.scalar.activation(result[:], acc[:], IDENTITY, bias=bias[:, block : block + 1])
-            else:
-                nc.vector.tensor_scalar(result[:], acc[:], bias[:, block : block + 1], None, op0=ADD)
-            nc.sync.dma_start(out[block * P : (block + 1) * P, piece * PIECE : (piece + 1) * PIECE], result[:])
+            for cut in range(n_cuts):
+                cols = slice(cut * width, (cut + 1) * width)
+                if block % 2 == 0:
+                    nc.scalar.activation(result[:, cols], acc[:, cols], IDENTITY, bias=bias[:, block : block + 1])
+                else:
+                    nc.vector.tensor_scalar(result[:, cols], acc[:, cols], bias[:, block : block + 1], None, op0=ADD)
+                first = piece * PIECE + cut * width
+                nc.sync.dma_start(out[block * P : (block + 1) * P, first : first + width], result[:, cols])
 
         tiles = [(piece, block) for piece in range(N_PIECES) for block in range(N_BLOCKS)]
         first, second = tiles[:BANKS], tiles[BANKS:]

@@ -10,6 +10,7 @@ V = 4096
 M = 512
 N = 2048
 PIECE = 512
+SIDE = PIECE // 2
 N_PIECES = N // PIECE
 N_BLOCKS = M // P
 BANKS = 8
@@ -21,7 +22,7 @@ def tile_sequencemodel_kernel(tc, table, w_tab, w_enc, b, t_time, t_f0, freq, ph
     nc = tc.nc
     with (
         tc.tile_pool(name="held", bufs=1) as held,
-        tc.tile_pool(name="times", bufs=2) as times,
+        tc.tile_pool(name="times", bufs=N_PIECES) as times,
         tc.tile_pool(name="encs", bufs=N_PIECES) as encs,
         tc.tile_pool(name="staged", bufs=BANKS) as staged,
         tc.psum_pool(name="banks", bufs=BANKS) as banks,
@@ -32,11 +33,11 @@ def tile_sequencemodel_kernel(tc, table, w_tab, w_enc, b, t_time, t_f0, freq, ph
         nc.sync.dma_start(offsets[:], offs)
         w_tab_sb = held.tile([P, M], BF16, name="w_tab_sb")
         nc.scalar.dma_start(w_tab_sb[:, 0:P], w_tab[:, 0:P])
-        freq_col = held.tile([P, 1], F32, name="freq_col")
-        nc.sync.dma_start(freq_col[:], freq)
-        phase_col = held.tile([P, 1], F32, name="phase_col")
-        nc.sync.dma_start(phase_col[:], phase)
         nc.sync.dma_start(w_tab_sb[:, P:M], w_tab[:, P:M])
+        freq_col = held.tile([P, 1], F32, name="freq_col")
+        nc.gpsimd.dma_start(freq_col[:], freq)
+        phase_col = held.tile([P, 1], F32, name="phase_col")
+        nc.gpsimd.dma_start(phase_col[:], phase)
         runs = held.tile([P, 2 * SQUARE], F32, name="runs", align_bytes=64)
         for group in range(P // SQUARE):
             source = t_time if group < 2 else t_f0
@@ -75,16 +76,14 @@ def tile_sequencemodel_kernel(tc, table, w_tab, w_enc, b, t_time, t_f0, freq, ph
             nc.tensor.matmul(acc[:], w_tab_sb[:, block * P : (block + 1) * P], looked_up, start=opens, stop=not opens)
 
         def enc_product(acc, enc, block, opens):
-            n_cuts = 1 if opens else 2
-            width = PIECE // n_cuts
-            for cut in range(n_cuts):
-                cols = slice(cut * width, (cut + 1) * width)
+            for side in range(2):
+                cols = slice(side * SIDE, (side + 1) * SIDE)
                 nc.tensor.matmul(
                     acc[:, cols],
                     w_enc_sb[:, block * P : (block + 1) * P],
                     enc[:, cols],
-                    start=opens,
-                    stop=not opens and cut == n_cuts - 1,
+                    start=opens and side == 0,
+                    stop=not opens and side == 1,
                 )
 
         def finish(acc, piece, block):
@@ -93,7 +92,7 @@ def tile_sequencemodel_kernel(tc, table, w_tab, w_enc, b, t_time, t_f0, freq, ph
             result = staged.tile([P, PIECE], F32, name="result")
             for cut in range(n_cuts):
                 cols = slice(cut * width, (cut + 1) * width)
-                if block % 2 == 0:
+                if block % 2 == 1:
                     nc.scalar.activation(result[:, cols], acc[:, cols], IDENTITY, bias=bias[:, block : block + 1])
                 else:
                     nc.vector.tensor_scalar(result[:, cols], acc[:, cols], bias[:, block : block + 1], None, op0=ADD)
@@ -101,18 +100,24 @@ def tile_sequencemodel_kernel(tc, table, w_tab, w_enc, b, t_time, t_f0, freq, ph
                 nc.sync.dma_start(out[block * P : (block + 1) * P, first : first + width], result[:, cols])
 
         tiles = [(piece, block) for piece in range(N_PIECES) for block in range(N_BLOCKS)]
-        first, second = tiles[:BANKS], tiles[BANKS:]
+        early, middle, late = tiles[: BANKS - 1], tiles[BANKS - 1 : 2 * BANKS - 1], tiles[2 * BANKS - 1 :]
         accs = {}
-        for piece, block in first:
-            accs[(piece, block)] = banks.tile([P, PIECE], F32, name="acc")
-            gathered_product(accs[(piece, block)], piece, block, opens=True)
+
+        def products(group, gathered, opens):
+            for piece, block in group:
+                if opens:
+                    accs[(piece, block)] = banks.tile([P, PIECE], F32, name="acc")
+                if gathered:
+                    gathered_product(accs[(piece, block)], piece, block, opens)
+                else:
+                    enc_product(accs[(piece, block)], encs_of[piece], block, opens)
+                if not opens:
+                    finish(accs[(piece, block)], piece, block)
+
+        products(early, gathered=True, opens=True)
         encs_of = [encode(piece) for piece in range(N_PIECES)]
-        for piece, block in first:
-            enc_product(accs[(piece, block)], encs_of[piece], block, opens=False)
-            finish(accs[(piece, block)], piece, block)
-        for piece, block in second:
-            accs[(piece, block)] = banks.tile([P, PIECE], F32, name="acc")
-            enc_product(accs[(piece, block)], encs_of[piece], block, opens=True)
-        for piece, block in second:
-            gathered_product(accs[(piece, block)], piece, block, opens=False)
-            finish(accs[(piece, block)], piece, block)
+        products(early, gathered=False, opens=False)
+        products(middle, gathered=False, opens=True)
+        products(middle, gathered=True, opens=False)
+        products(late, gathered=True, opens=True)
+        products(late, gathered=False, opens=False)

@@ -87,17 +87,12 @@ def tile_sequencemodel_kernel(tc, table, w_tab, w_enc, b, t_time, t_f0, freq, ph
                 )
 
         def finish(acc, piece, block):
-            n_cuts = 2 if (piece, block) == (N_PIECES - 1, N_BLOCKS - 1) else 1
-            width = PIECE // n_cuts
             result = staged.tile([P, PIECE], F32, name="result")
-            for cut in range(n_cuts):
-                cols = slice(cut * width, (cut + 1) * width)
-                if block % 2 == 1:
-                    nc.scalar.activation(result[:, cols], acc[:, cols], IDENTITY, bias=bias[:, block : block + 1])
-                else:
-                    nc.vector.tensor_scalar(result[:, cols], acc[:, cols], bias[:, block : block + 1], None, op0=ADD)
-                first = piece * PIECE + cut * width
-                nc.sync.dma_start(out[block * P : (block + 1) * P, first : first + width], result[:, cols])
+            if block % 2 == 1:
+                nc.scalar.activation(result[:], acc[:], IDENTITY, bias=bias[:, block : block + 1])
+            else:
+                nc.vector.tensor_scalar(result[:], acc[:], bias[:, block : block + 1], None, op0=ADD)
+            nc.sync.dma_start(out[block * P : (block + 1) * P, piece * PIECE : (piece + 1) * PIECE], result[:])
 
         tiles = [(piece, block) for piece in range(N_PIECES) for block in range(N_BLOCKS)]
         early, middle, late = tiles[: BANKS - 1], tiles[BANKS - 1 : 2 * BANKS - 1], tiles[2 * BANKS - 1 :]

@@ -24,7 +24,7 @@ def tile_sequencemodel_kernel(tc, table, w_tab, w_enc, b, t_time, t_f0, freq, ph
         tc.tile_pool(name="held", bufs=1) as held,
         tc.tile_pool(name="times", bufs=N_PIECES) as times,
         tc.tile_pool(name="encs", bufs=N_PIECES) as encs,
-        tc.tile_pool(name="staged", bufs=BANKS) as staged,
+        tc.tile_pool(name="staged", bufs=N_PIECES * N_BLOCKS) as staged,
         tc.psum_pool(name="banks", bufs=BANKS) as banks,
     ):
         table_sb = held.tile([P, V], BF16, name="table_sb")

import concourse.mybir as mybir

BF16, F32, U16 = mybir.dt.bfloat16, mybir.dt.float32, mybir.dt.uint16
ADD = mybir.AluOpType.add
SIN, IDENTITY = mybir.ActivationFunctionType.Sin, mybir.ActivationFunctionType.Identity

P = 128
SQUARE = 32
V = 4096
M = 512
N = 2048
PIECE = 512
SIDE = PIECE // 2
N_PIECES = N // PIECE
N_BLOCKS = M // P
BANKS = 8

FLOPS = 2 * (P + P) * M * N


def tile_sequencemodel_kernel(tc, table, w_tab, w_enc, b, t_time, t_f0, freq, phase, offs, out):
    nc = tc.nc
    with (
        tc.tile_pool(name="held", bufs=1) as held,
        tc.tile_pool(name="times", bufs=N_PIECES) as times,
        tc.tile_pool(name="encs", bufs=N_PIECES) as encs,
        tc.tile_pool(name="staged", bufs=N_PIECES * N_BLOCKS) as staged,
        tc.psum_pool(name="banks", bufs=BANKS) as banks,
    ):
        table_sb = held.tile([P, V], BF16, name="table_sb")
        nc.sync.dma_start(table_sb[:], table)
        offsets = held.tile([P, N // 16], U16, name="offsets")
        nc.sync.dma_start(offsets[:], offs)
        w_tab_sb = held.tile([P, M], BF16, name="w_tab_sb")
        nc.scalar.dma_start(w_tab_sb[:, 0:P], w_tab[:, 0:P])
        nc.sync.dma_start(w_tab_sb[:, P:M], w_tab[:, P:M])
        freq_col = held.tile([P, 1], F32, name="freq_col")
        nc.gpsimd.dma_start(freq_col[:], freq)
        phase_col = held.tile([P, 1], F32, name="phase_col")
        nc.gpsimd.dma_start(phase_col[:], phase)
        runs = held.tile([P, 2 * SQUARE], F32, name="runs", align_bytes=64)
        for group in range(P // SQUARE):
            source = t_time if group < 2 else t_f0
            nc.sync.dma_start(
                runs[group * SQUARE : (group + 1) * SQUARE, :].rearrange("a (h r) -> a h r", h=2),
                source.rearrange("one (h a r) -> (one a) h r", h=2, a=SQUARE),
            )
        w_enc_sb = held.tile([P, M], BF16, name="w_enc_sb")
        nc.sync.dma_start(w_enc_sb[:], w_enc)
        bias = held.tile([P, N_BLOCKS], F32, name="bias")
        nc.sync.dma_start(bias[:], b.rearrange("(block p) one -> p (block one)", p=P))

        turned = held.tile([P, 2 * SQUARE], F32, name="turned", align_bytes=64)
        for h in range(2):
            cols = slice(h * SQUARE, (h + 1) * SQUARE)
            nc.vector.transpose(turned[:, cols], runs[:, cols])

        def spread(piece):
            n_runs = PIECE // SQUARE
            repeated = times.tile([P, PIECE], F32, name="repeated", align_bytes=64)
            nc.vector.tensor_copy(
                repeated[:].rearrange("p (c s) -> p c s", s=SQUARE),
                turned[:, piece * n_runs : (piece + 1) * n_runs].unsqueeze(2).to_broadcast([P, n_runs, SQUARE]),
            )
            tt = times.tile([P, PIECE], F32, name="tt", align_bytes=64)
            nc.vector.transpose(tt[:], repeated[:])
            return tt

        def encode(piece):
            enc = encs.tile([P, PIECE], BF16, name="enc")
            nc.scalar.activation(enc[:], spread(piece)[:], SIN, bias=phase_col[:], scale=freq_col[:])
            return enc

        def gathered_product(acc, piece, block, opens):
            looked_up = table_sb[:].indirect(offsets[:, piece * (PIECE // 16) : (piece + 1) * (PIECE // 16)])
            nc.tensor.matmul(acc[:], w_tab_sb[:, block * P : (block + 1) * P], looked_up, start=opens, stop=not opens)

        def enc_product(acc, enc, block, opens):
            for side in range(2):
                cols = slice(side * SIDE, (side + 1) * SIDE)
                nc.tensor.matmul(
                    acc[:, cols],
                    w_enc_sb[:, block * P : (block + 1) * P],
                    enc[:, cols],
                    start=opens and side == 0,
                    stop=not opens and side == 1,
                )

        def finish(acc, piece, block):
            result = staged.tile([P, PIECE], F32, name="result")
            if block % 2 == 1:
                nc.scalar.activation(result[:], acc[:], IDENTITY, bias=bias[:, block : block + 1])
            else:
                nc.vector.tensor_scalar(result[:], acc[:], bias[:, block : block + 1], None, op0=ADD)
            nc.sync.dma_start(out[block * P : (block + 1) * P, piece * PIECE : (piece + 1) * PIECE], result[:])

        tiles = [(piece, block) for piece in range(N_PIECES) for block in range(N_BLOCKS)]
        early, middle, late = tiles[: BANKS - 1], tiles[BANKS - 1 : 2 * BANKS - 1], tiles[2 * BANKS - 1 :]
        accs = {}

        def products(group, gathered, opens):
            for piece, block in group:
                if opens:
                    accs[(piece, block)] = banks.tile([P, PIECE], F32, name="acc")
                if gathered:
                    gathered_product(accs[(piece, block)], piece, block, opens)
                else:
                    enc_product(accs[(piece, block)], encs_of[piece], block, opens)
                if not opens:
                    finish(accs[(piece, block)], piece, block)

        products(early, gathered=True, opens=True)
        encs_of = [encode(piece) for piece in range(N_PIECES)]
        products(early, gathered=False, opens=False)
        products(middle, gathered=False, opens=True)
        products(middle, gathered=True, opens=False)
        products(late, gathered=True, opens=True)
        products(late, gathered=False, opens=False)
